import numpy as np
import ml_dtypes

BF16 = ml_dtypes.bfloat16


def bf(x):
    return np.asarray(x, np.float32).astype(BF16)


def f32(x):
    return np.asarray(x, np.float32)


def f64(x):
    return np.asarray(x).astype(np.float64)


def striped(idx):
    return np.tile(idx.reshape(-1, 16).T, (8, 1))


S, L, D, M, H, HD, NQ, T, N, R = 1024, 128, 128, 256, 2, 64, 128, 16, 2048, 2
SCALE = 1.0 / np.sqrt(HD)


def setup_inputs():
    return {"table": bf(np.random.standard_normal((L, S))), "w": bf(np.random.standard_normal((L, M)) / np.sqrt(L)), "x_q": bf(np.random.standard_normal((D, NQ))), "w_q": bf(np.random.standard_normal((D, D)) / np.sqrt(D)), "offs": striped(np.concatenate([np.random.permutation(S) for _ in range(R)]))}


def reference(table, w, x_q, w_q, offs):
    idx = offs[:16].T.reshape(-1)
    kv = f64(w).T @ f64(table)[:, idx]
    key = kv[:D].reshape(H, HD, NQ, T)
    val = kv[D:].reshape(H, HD, NQ, T)
    q = (f64(w_q).T @ f64(x_q)).reshape(H, HD, NQ)
    score = SCALE * np.sum(q[:, :, :, None] * key, axis=1)
    e = np.exp(score - score.max(axis=-1, keepdims=True))
    attn = e / e.sum(axis=-1, keepdims=True)
    o = np.sum(attn[:, None, :, :] * val, axis=-1)
    return o.reshape(D, NQ)

@@ -1,0 +1,97 @@
+import concourse.mybir as mybir
+
+BF16, F32, U16 = mybir.dt.bfloat16, mybir.dt.float32, mybir.dt.uint16
+ALU = mybir.AluOpType
+EXP = mybir.ActivationFunctionType.Exp
+X = mybir.AxisListType.X
+
+P = 128
+PLACES = 1024
+QUERIES = 128
+T = 16
+HEAD = 64
+PIECE = 512
+PIECE_Q = PIECE // T
+PIECES = QUERIES // PIECE_Q
+SCALE = 0.125
+
+FLOPS = 2 * P * 2 * P * QUERIES * T + 2 * P * P * QUERIES + 4 * P * QUERIES * T
+
+
+def tile_deepseekmla_kernel(tc, table, w, x_q, w_q, offs, out):
+    nc = tc.nc
+    with (
+        tc.tile_pool(name="held", bufs=1) as held,
+        tc.tile_pool(name="work", bufs=2) as work,
+        tc.psum_pool(name="psum", bufs=8) as psum,
+    ):
+        offsets = held.tile([P, QUERIES], U16, name="offsets")
+        nc.sync.dma_start(offsets[:], offs)
+        table_sb = held.tile([P, PLACES], BF16, name="table_sb")
+        nc.sync.dma_start(table_sb[:], table)
+        w_sb = held.tile([P, 2 * P], BF16, name="w_sb")
+        nc.scalar.dma_start(w_sb[:], w)
+        w_q_sb = held.tile([P, P], BF16, name="w_q_sb")
+        nc.scalar.dma_start(w_q_sb[:], w_q)
+        x_q_sb = held.tile([P, QUERIES], BF16, name="x_q_sb")
+        nc.scalar.dma_start(x_q_sb[:], x_q)
+
+        head_sum = held.tile([P, P], BF16, name="head_sum")
+        nc.gpsimd.memset(head_sum[:], 0.0)
+        nc.gpsimd.memset(head_sum[0:HEAD, 0:HEAD], SCALE)
+        nc.gpsimd.memset(head_sum[HEAD:P, HEAD:P], SCALE)
+
+        q_ps = psum.tile([P, QUERIES], F32, name="q_ps", tag="bank")
+        nc.tensor.matmul(q_ps[:], w_q_sb[:], x_q_sb[:])
+        q_sb = held.tile([P, QUERIES], F32, name="q_sb")
+        nc.vector.tensor_copy(q_sb[:], q_ps[:])
+
+        key_ps, val_ps = [], []
+        for half, banks in ((0, key_ps), (1, val_ps)):
+            for p in range(PIECES):
+                bank = psum.tile([P, PIECE], F32, name=f"kv{half}_{p}", tag="bank")
+                nc.tensor.matmul(
+                    bank[:],
+                    w_sb[:, half * P : (half + 1) * P],
+                    table_sb[:].indirect(offsets[:, p * PIECE_Q : (p + 1) * PIECE_Q]),
+                )
+                banks.append(bank)
+
+        out_sb = held.tile([P, QUERIES], F32, name="out_sb")
+        for p in range(PIECES):
+            queries = slice(p * PIECE_Q, (p + 1) * PIECE_Q)
+            by_query = [P, PIECE_Q, T]
+
+            prod = work.tile(by_query, BF16, name="prod")
+            nc.vector.tensor_tensor(
+                prod[:],
+                key_ps[p][:].rearrange("c (i t) -> c i t", t=T),
+                q_sb[:, queries].unsqueeze(2).to_broadcast(by_query),
+                ALU.mult,
+            )
+            score_ps = psum.tile([P, PIECE], F32, name="score_ps", tag="bank")
+            nc.tensor.matmul(score_ps[:], head_sum[:], prod[:].rearrange("c i t -> c (i t)"))
+            score = score_ps[:].rearrange("c (i t) -> c i t", t=T)
+
+            top = work.tile([P, PIECE_Q], F32, name="top")
+            nc.vector.tensor_reduce(top[:], score, X, ALU.max)
+            shifted = work.tile(by_query, F32, name="shifted")
+            nc.vector.tensor_tensor(
+                shifted[:], score, top[:].unsqueeze(2).to_broadcast(by_query), ALU.subtract
+            )
+
+            terms = work.tile([P, 2, PIECE_Q, T], F32, name="terms")
+            nc.scalar.activation(terms[:, 0], shifted[:], EXP)
+            nc.vector.tensor_tensor(
+                terms[:, 1],
+                val_ps[p][:].rearrange("c (i t) -> c i t", t=T),
+                terms[:, 0],
+                ALU.mult,
+            )
+            sums = work.tile([P, 2, PIECE_Q], F32, name="sums")
+            nc.vector.tensor_reduce(sums[:], terms[:], X, ALU.add)
+            inv = work.tile([P, PIECE_Q], F32, name="inv")
+            nc.vector.reciprocal(inv[:], sums[:, 0])
+            nc.vector.tensor_tensor(out_sb[:, queries], sums[:, 1], inv[:], ALU.mult)
+
+        nc.sync.dma_start(out, out_sb[:])

@@ -1,4 +1,5 @@
 import concourse.mybir as mybir
+from concourse.masks import make_identity
 
 BF16, F32, U16 = mybir.dt.bfloat16, mybir.dt.float32, mybir.dt.uint16
 ALU = mybir.AluOpType
@@ -9,6 +10,7 @@ P = 128
 PLACES = 1024
 QUERIES = 128
 T = 16
+HEADS = 2
 HEAD = 64
 PIECE = 512
 PIECE_Q = PIECE // T
@@ -40,6 +42,9 @@ def tile_deepseekmla_kernel(tc, table, w, x_q, w_q, offs, out):
         nc.gpsimd.memset(head_sum[:], 0.0)
         nc.gpsimd.memset(head_sum[0:HEAD, 0:HEAD], SCALE)
         nc.gpsimd.memset(head_sum[HEAD:P, HEAD:P], SCALE)
+        head_pick = head_sum[:].rearrange("c (h k) -> c h k", k=HEAD)[:, :, 0]
+        ident = held.tile([P, P], F32, name="ident")
+        make_identity(nc, ident[:])
 
         q_ps = psum.tile([P, QUERIES], F32, name="q_ps", tag="bank")
         nc.tensor.matmul(q_ps[:], w_q_sb[:], x_q_sb[:])
@@ -57,41 +62,69 @@ def tile_deepseekmla_kernel(tc, table, w, x_q, w_q, offs, out):
                 )
                 banks.append(bank)
 
-        out_sb = held.tile([P, QUERIES], F32, name="out_sb")
+        by_query = [P, PIECE_Q, T]
+        prod = held.tile([P, QUERIES, T], BF16, name="prod")
         for p in range(PIECES):
             queries = slice(p * PIECE_Q, (p + 1) * PIECE_Q)
-            by_query = [P, PIECE_Q, T]
-
-            prod = work.tile(by_query, BF16, name="prod")
             nc.vector.tensor_tensor(
-                prod[:],
+                prod[:, queries, :],
                 key_ps[p][:].rearrange("c (i t) -> c i t", t=T),
                 q_sb[:, queries].unsqueeze(2).to_broadcast(by_query),
                 ALU.mult,
             )
-            score_ps = psum.tile([P, PIECE], F32, name="score_ps", tag="bank")
-            nc.tensor.matmul(score_ps[:], head_sum[:], prod[:].rearrange("c i t -> c (i t)"))
-            score = score_ps[:].rearrange("c (i t) -> c i t", t=T)
 
-            top = work.tile([P, PIECE_Q], F32, name="top")
-            nc.vector.tensor_reduce(top[:], score, X, ALU.max)
-            shifted = work.tile(by_query, F32, name="shifted")
-            nc.vector.tensor_tensor(
-                shifted[:], score, top[:].unsqueeze(2).to_broadcast(by_query), ALU.subtract
+        own_ps = psum.tile([P, T, HEADS], F32, name="own_ps", tag="bank")
+        for t in range(T):
+            nc.tensor.matmul(own_ps[:, t, :], prod[:, :, t], head_pick)
+        own = own_ps[:].rearrange("i t h -> i h t")
+        per_channel = [P, HEADS, HEAD]
+
+        top = held.tile([P, HEADS], F32, name="top")
+        nc.vector.tensor_reduce(top[:], own, X, ALU.max)
+        minus_top = held.tile([P, P], F32, name="minus_top")
+        nc.vector.tensor_scalar_mul(
+            minus_top[:].rearrange("i (h k) -> i h k", k=HEAD),
+            top[:].unsqueeze(2).to_broadcast(per_channel),
+            -1.0,
+        )
+        centred = held.tile([P, HEADS, T], F32, name="centred")
+        nc.vector.tensor_tensor(
+            centred[:], own, top[:].unsqueeze(2).to_broadcast([P, HEADS, T]), ALU.subtract
+        )
+        own_exp = held.tile([P, HEADS, T], F32, name="own_exp")
+        nc.scalar.activation(own_exp[:], centred[:], EXP)
+        total = held.tile([P, HEADS], F32, name="total")
+        nc.vector.tensor_reduce(total[:], own_exp[:], X, ALU.add)
+        inv = held.tile([P, HEADS], F32, name="inv")
+        nc.vector.reciprocal(inv[:], total[:])
+        inv_wide = held.tile([P, P], F32, name="inv_wide")
+        nc.vector.tensor_copy(
+            inv_wide[:].rearrange("i (h k) -> i h k", k=HEAD),
+            inv[:].unsqueeze(2).to_broadcast(per_channel),
+        )
+
+        mix = held.tile([P, QUERIES], F32, name="mix")
+        for p in range(PIECES):
+            queries = slice(p * PIECE_Q, (p + 1) * PIECE_Q)
+            score_ps = psum.tile(by_query, F32, name="score_ps", tag="bank")
+            nc.tensor.matmul(score_ps[:], head_sum[:], prod[:, queries, :], start=True, stop=False)
+            nc.tensor.matmul(
+                score_ps[:],
+                minus_top[:],
+                ident[:, queries].unsqueeze(2).to_broadcast(by_query),
+                start=False,
+                stop=True,
             )
-
-            terms = work.tile([P, 2, PIECE_Q, T], F32, name="terms")
-            nc.scalar.activation(terms[:, 0], shifted[:], EXP)
+            weight = work.tile(by_query, F32, name="weight")
+            nc.scalar.activation(weight[:], score_ps[:], EXP)
+            terms = work.tile(by_query, F32, name="terms")
             nc.vector.tensor_tensor(
-                terms[:, 1],
-                val_ps[p][:].rearrange("c (i t) -> c i t", t=T),
-                terms[:, 0],
-                ALU.mult,
+                terms[:], val_ps[p][:].rearrange("c (i t) -> c i t", t=T), weight[:], ALU.mult
             )
-            sums = work.tile([P, 2, PIECE_Q], F32, name="sums")
-            nc.vector.tensor_reduce(sums[:], terms[:], X, ALU.add)
-            inv = work.tile([P, PIECE_Q], F32, name="inv")
-            nc.vector.reciprocal(inv[:], sums[:, 0])
-            nc.vector.tensor_tensor(out_sb[:, queries], sums[:, 1], inv[:], ALU.mult)
+            nc.vector.tensor_reduce(mix[:, queries], terms[:], X, ALU.add)
 
+        inv_ps = psum.tile([P, QUERIES], F32, name="inv_ps", tag="bank")
+        nc.tensor.matmul(inv_ps[:], inv_wide[:], ident[:])
+        out_sb = held.tile([P, QUERIES], F32, name="out_sb")
+        nc.vector.tensor_tensor(out_sb[:], mix[:], inv_ps[:], ALU.mult)
         nc.sync.dma_start(out, out_sb[:])

@@ -81,12 +81,15 @@ def tile_deepseekmla_kernel(tc, table, w, x_q, w_q, offs, out):
 
         top = held.tile([P, HEADS], F32, name="top")
         nc.vector.tensor_reduce(top[:], own, X, ALU.max)
-        minus_top = held.tile([P, P], F32, name="minus_top")
-        nc.vector.tensor_scalar_mul(
-            minus_top[:].rearrange("i (h k) -> i h k", k=HEAD),
+        top_wide = held.tile([P, P], F32, name="top_wide")
+        nc.vector.tensor_copy(
+            top_wide[:].rearrange("i (h k) -> i h k", k=HEAD),
             top[:].unsqueeze(2).to_broadcast(per_channel),
-            -1.0,
         )
+        top_ps = psum.tile([P, QUERIES], F32, name="top_ps", tag="bank")
+        nc.tensor.matmul(top_ps[:], top_wide[:], ident[:])
+        top_sb = held.tile([P, QUERIES], F32, name="top_sb")
+        nc.scalar.copy(top_sb[:], top_ps[:])
         centred = held.tile([P, HEADS, T], F32, name="centred")
         nc.vector.tensor_tensor(
             centred[:], own, top[:].unsqueeze(2).to_broadcast([P, HEADS, T]), ALU.subtract
@@ -107,16 +110,16 @@ def tile_deepseekmla_kernel(tc, table, w, x_q, w_q, offs, out):
         for p in range(PIECES):
             queries = slice(p * PIECE_Q, (p + 1) * PIECE_Q)
             score_ps = psum.tile(by_query, F32, name="score_ps", tag="bank")
-            nc.tensor.matmul(score_ps[:], head_sum[:], prod[:, queries, :], start=True, stop=False)
-            nc.tensor.matmul(
+            nc.tensor.matmul(score_ps[:], head_sum[:], prod[:, queries, :])
+            shifted = work.tile(by_query, F32, name="shifted")
+            nc.vector.tensor_tensor(
+                shifted[:],
                 score_ps[:],
-                minus_top[:],
-                ident[:, queries].unsqueeze(2).to_broadcast(by_query),
-                start=False,
-                stop=True,
+                top_sb[:, queries].unsqueeze(2).to_broadcast(by_query),
+                ALU.subtract,
             )
             weight = work.tile(by_query, F32, name="weight")
-            nc.scalar.activation(weight[:], score_ps[:], EXP)
+            nc.scalar.activation(weight[:], shifted[:], EXP)
             terms = work.tile(by_query, F32, name="terms")
             nc.vector.tensor_tensor(
                 terms[:], val_ps[p][:].rearrange("c (i t) -> c i t", t=T), weight[:], ALU.mult

@@ -10,6 +10,7 @@ P = 128
 PLACES = 1024
 QUERIES = 128
 T = 16
+T_OUT, T_IN = 4, 4
 HEADS = 2
 HEAD = 64
 PIECE = 512
@@ -63,33 +64,35 @@ def tile_deepseekmla_kernel(tc, table, w, x_q, w_q, offs, out):
                 banks.append(bank)
 
         by_query = [P, PIECE_Q, T]
-        prod = held.tile([P, QUERIES, T], BF16, name="prod")
+        prod = held.tile([P, T_OUT, QUERIES, T_IN], BF16, name="prod")
+        split_t = [P, PIECE_Q, T_OUT, T_IN]
+
+        def prod_of(queries):
+            return prod[:, :, queries, :].rearrange("c a i b -> c i a b")
+
         for p in range(PIECES):
             queries = slice(p * PIECE_Q, (p + 1) * PIECE_Q)
             nc.vector.tensor_tensor(
-                prod[:, queries, :],
-                key_ps[p][:].rearrange("c (i t) -> c i t", t=T),
-                q_sb[:, queries].unsqueeze(2).to_broadcast(by_query),
+                prod_of(queries),
+                key_ps[p][:].rearrange("c (i a b) -> c i a b", a=T_OUT, b=T_IN),
+                q_sb[:, queries].unsqueeze(2).unsqueeze(3).to_broadcast(split_t),
                 ALU.mult,
             )
 
         own_ps = psum.tile([P, T, HEADS], F32, name="own_ps", tag="bank")
         for t in range(T):
-            nc.tensor.matmul(own_ps[:, t, :], prod[:, :, t], head_pick)
+            nc.tensor.matmul(own_ps[:, t, :], prod[:, t // T_IN, :, t % T_IN], head_pick)
         own = own_ps[:].rearrange("i t h -> i h t")
         per_channel = [P, HEADS, HEAD]
 
         top = held.tile([P, HEADS], F32, name="top")
         nc.vector.tensor_reduce(top[:], own, X, ALU.max)
-        top_wide = held.tile([P, P], F32, name="top_wide")
-        nc.vector.tensor_copy(
-            top_wide[:].rearrange("i (h k) -> i h k", k=HEAD),
+        minus_top = held.tile([P, P], F32, name="minus_top")
+        nc.vector.tensor_scalar_mul(
+            minus_top[:].rearrange("i (h k) -> i h k", k=HEAD),
             top[:].unsqueeze(2).to_broadcast(per_channel),
+            -1.0,
         )
-        top_ps = psum.tile([P, QUERIES], F32, name="top_ps", tag="bank")
-        nc.tensor.matmul(top_ps[:], top_wide[:], ident[:])
-        top_sb = held.tile([P, QUERIES], F32, name="top_sb")
-        nc.scalar.copy(top_sb[:], top_ps[:])
         centred = held.tile([P, HEADS, T], F32, name="centred")
         nc.vector.tensor_tensor(
             centred[:], own, top[:].unsqueeze(2).to_broadcast([P, HEADS, T]), ALU.subtract
@@ -110,16 +113,22 @@ def tile_deepseekmla_kernel(tc, table, w, x_q, w_q, offs, out):
         for p in range(PIECES):
             queries = slice(p * PIECE_Q, (p + 1) * PIECE_Q)
             score_ps = psum.tile(by_query, F32, name="score_ps", tag="bank")
-            nc.tensor.matmul(score_ps[:], head_sum[:], prod[:, queries, :])
-            shifted = work.tile(by_query, F32, name="shifted")
-            nc.vector.tensor_tensor(
-                shifted[:],
+            nc.tensor.matmul(
+                score_ps[:].rearrange("c i (a b) -> c i a b", a=T_OUT),
+                head_sum[:],
+                prod_of(queries),
+                start=True,
+                stop=False,
+            )
+            nc.tensor.matmul(
                 score_ps[:],
-                top_sb[:, queries].unsqueeze(2).to_broadcast(by_query),
-                ALU.subtract,
+                minus_top[:],
+                ident[:, queries].unsqueeze(2).to_broadcast(by_query),
+                start=False,
+                stop=True,
             )
             weight = work.tile(by_query, F32, name="weight")
-            nc.scalar.activation(weight[:], shifted[:], EXP)
+            nc.scalar.activation(weight[:], score_ps[:], EXP)
             terms = work.tile(by_query, F32, name="terms")
             nc.vector.tensor_tensor(
                 terms[:], val_ps[p][:].rearrange("c (i t) -> c i t", t=T), weight[:], ALU.mult

@@ -16,6 +16,7 @@ HEAD = 64
 PIECE = 512
 PIECE_Q = PIECE // T
 PIECES = QUERIES // PIECE_Q
+CHUNK_Q = 16
 SCALE = 0.125
 
 FLOPS = 2 * P * 2 * P * QUERIES * T + 2 * P * P * QUERIES + 4 * P * QUERIES * T
@@ -25,7 +26,6 @@ def tile_deepseekmla_kernel(tc, table, w, x_q, w_q, offs, out):
     nc = tc.nc
     with (
         tc.tile_pool(name="held", bufs=1) as held,
-        tc.tile_pool(name="work", bufs=2) as work,
         tc.psum_pool(name="psum", bufs=8) as psum,
     ):
         offsets = held.tile([P, QUERIES], U16, name="offsets")
@@ -79,6 +79,11 @@ def tile_deepseekmla_kernel(tc, table, w, x_q, w_q, offs, out):
                 ALU.mult,
             )
 
+        val = held.tile([P, QUERIES, T], F32, name="val")
+        for p in range(PIECES):
+            queries = slice(p * PIECE_Q, (p + 1) * PIECE_Q)
+            nc.scalar.copy(val[:, queries, :], val_ps[p][:].rearrange("c (i t) -> c i t", t=T))
+
         own_ps = psum.tile([P, T, HEADS], F32, name="own_ps", tag="bank")
         for t in range(T):
             nc.tensor.matmul(own_ps[:, t, :], prod[:, t // T_IN, :, t % T_IN], head_pick)
@@ -109,10 +114,12 @@ def tile_deepseekmla_kernel(tc, table, w, x_q, w_q, offs, out):
             inv[:].unsqueeze(2).to_broadcast(per_channel),
         )
 
+        weight = held.tile([P, QUERIES, T], F32, name="weight")
+        terms = held.tile([P, QUERIES, T], F32, name="terms")
         mix = held.tile([P, QUERIES], F32, name="mix")
-        for p in range(PIECES):
-            queries = slice(p * PIECE_Q, (p + 1) * PIECE_Q)
-            score_ps = psum.tile(by_query, F32, name="score_ps", tag="bank")
+        chunks = [slice(k * CHUNK_Q, (k + 1) * CHUNK_Q) for k in range(QUERIES // CHUNK_Q)]
+        for k, queries in enumerate(chunks):
+            score_ps = psum.tile([P, CHUNK_Q, T], F32, name="score_ps", tag="bank")
             nc.tensor.matmul(
                 score_ps[:].rearrange("c i (a b) -> c i a b", a=T_OUT),
                 head_sum[:],
@@ -123,17 +130,15 @@ def tile_deepseekmla_kernel(tc, table, w, x_q, w_q, offs, out):
             nc.tensor.matmul(
                 score_ps[:],
                 minus_top[:],
-                ident[:, queries].unsqueeze(2).to_broadcast(by_query),
+                ident[:, queries].unsqueeze(2).to_broadcast([P, CHUNK_Q, T]),
                 start=False,
                 stop=True,
             )
-            weight = work.tile(by_query, F32, name="weight")
-            nc.scalar.activation(weight[:], score_ps[:], EXP)
-            terms = work.tile(by_query, F32, name="terms")
+            nc.scalar.activation(weight[:, queries, :], score_ps[:], EXP)
             nc.vector.tensor_tensor(
-                terms[:], val_ps[p][:].rearrange("c (i t) -> c i t", t=T), weight[:], ALU.mult
+                terms[:, queries, :], val[:, queries, :], weight[:, queries, :], ALU.mult
             )
-            nc.vector.tensor_reduce(mix[:, queries], terms[:], X, ALU.add)
+            nc.vector.tensor_reduce(mix[:, queries], terms[:, queries, :], X, ALU.add)
 
         inv_ps = psum.tile([P, QUERIES], F32, name="inv_ps", tag="bank")
         nc.tensor.matmul(inv_ps[:], inv_wide[:], ident[:])

@@ -79,6 +79,13 @@ def tile_deepseekmla_kernel(tc, table, w, x_q, w_q, offs, out):
                 ALU.mult,
             )
 
+        prod_t = held.tile([P, T, QUERIES], BF16, name="prod_t")
+        for p in range(PIECES):
+            queries = slice(p * PIECE_Q, (p + 1) * PIECE_Q)
+            nc.scalar.copy(
+                prod_t[:, :, queries].rearrange("c (a b) i -> c a b i", a=T_OUT),
+                prod[:, :, queries, :].rearrange("c a i b -> c a b i"),
+            )
         val = held.tile([P, QUERIES, T], F32, name="val")
         for p in range(PIECES):
             queries = slice(p * PIECE_Q, (p + 1) * PIECE_Q)
@@ -86,7 +93,7 @@ def tile_deepseekmla_kernel(tc, table, w, x_q, w_q, offs, out):
 
         own_ps = psum.tile([P, T, HEADS], F32, name="own_ps", tag="bank")
         for t in range(T):
-            nc.tensor.matmul(own_ps[:, t, :], prod[:, t // T_IN, :, t % T_IN], head_pick)
+            nc.tensor.matmul(own_ps[:, t, :], prod_t[:, t, :], head_pick)
         own = own_ps[:].rearrange("i t h -> i h t")
         per_channel = [P, HEADS, HEAD]
 

@@ -46,6 +46,8 @@ def tile_deepseekmla_kernel(tc, table, w, x_q, w_q, offs, out):
         head_pick = head_sum[:].rearrange("c (h k) -> c h k", k=HEAD)[:, :, 0]
         ident = held.tile([P, P], F32, name="ident")
         make_identity(nc, ident[:])
+        ident_bf = held.tile([P, P], BF16, name="ident_bf")
+        make_identity(nc, ident_bf[:])
 
         q_ps = psum.tile([P, QUERIES], F32, name="q_ps", tag="bank")
         nc.tensor.matmul(q_ps[:], w_q_sb[:], x_q_sb[:])
@@ -99,16 +101,15 @@ def tile_deepseekmla_kernel(tc, table, w, x_q, w_q, offs, out):
 
         top = held.tile([P, HEADS], F32, name="top")
         nc.vector.tensor_reduce(top[:], own, X, ALU.max)
-        minus_top = held.tile([P, P], F32, name="minus_top")
+        minus_top = held.tile([P, P], BF16, name="minus_top")
         nc.vector.tensor_scalar_mul(
             minus_top[:].rearrange("i (h k) -> i h k", k=HEAD),
             top[:].unsqueeze(2).to_broadcast(per_channel),
             -1.0,
         )
         centred = held.tile([P, HEADS, T], F32, name="centred")
-        nc.vector.tensor_tensor(
-            centred[:], own, top[:].unsqueeze(2).to_broadcast([P, HEADS, T]), ALU.subtract
-        )
+        shift = minus_top[:].rearrange("i (h k) -> i h k", k=HEAD)[:, :, 0:1]
+        nc.vector.tensor_tensor(centred[:], own, shift.to_broadcast([P, HEADS, T]), ALU.add)
         own_exp = held.tile([P, HEADS, T], F32, name="own_exp")
         nc.scalar.activation(own_exp[:], centred[:], EXP)
         total = held.tile([P, HEADS], F32, name="total")
@@ -137,7 +138,7 @@ def tile_deepseekmla_kernel(tc, table, w, x_q, w_q, offs, out):
             nc.tensor.matmul(
                 score_ps[:],
                 minus_top[:],
-                ident[:, queries].unsqueeze(2).to_broadcast([P, CHUNK_Q, T]),
+                ident_bf[:, queries].unsqueeze(2).to_broadcast([P, CHUNK_Q, T]),
                 start=False,
                 stop=True,
             )

@@ -126,7 +126,8 @@ def tile_deepseekmla_kernel(tc, table, w, x_q, w_q, offs, out):
         terms = held.tile([P, QUERIES, T], F32, name="terms")
         mix = held.tile([P, QUERIES], F32, name="mix")
         chunks = [slice(k * CHUNK_Q, (k + 1) * CHUNK_Q) for k in range(QUERIES // CHUNK_Q)]
-        for k, queries in enumerate(chunks):
+
+        def weigh(queries):
             score_ps = psum.tile([P, CHUNK_Q, T], F32, name="score_ps", tag="bank")
             nc.tensor.matmul(
                 score_ps[:].rearrange("c i (a b) -> c i a b", a=T_OUT),
@@ -143,6 +144,22 @@ def tile_deepseekmla_kernel(tc, table, w, x_q, w_q, offs, out):
                 stop=True,
             )
             nc.scalar.activation(weight[:, queries, :], score_ps[:], EXP)
+
+        for queries in chunks[: PIECE_Q // CHUNK_Q]:
+            weigh(queries)
+        first = slice(0, PIECE_Q)
+        nc.gpsimd.tensor_tensor(terms[:, first, :], val[:, first, :], weight[:, first, :], ALU.mult)
+        for width in (T // 2, T // 4, T // 8):
+            nc.gpsimd.tensor_tensor(
+                terms[:, first, 0:width],
+                terms[:, first, 0:width],
+                terms[:, first, width : 2 * width],
+                ALU.add,
+            )
+        nc.gpsimd.tensor_tensor(mix[:, first], terms[:, first, 0], terms[:, first, 1], ALU.add)
+
+        for queries in chunks[PIECE_Q // CHUNK_Q :]:
+            weigh(queries)
             nc.vector.tensor_tensor(
                 terms[:, queries, :], val[:, queries, :], weight[:, queries, :], ALU.mult
             )

@@ -88,10 +88,13 @@ def tile_deepseekmla_kernel(tc, table, w, x_q, w_q, offs, out):
                 prod_t[:, :, queries].rearrange("c (a b) i -> c a b i", a=T_OUT),
                 prod[:, :, queries, :].rearrange("c a i b -> c a b i"),
             )
-        val = held.tile([P, QUERIES, T], F32, name="val")
-        for p in range(PIECES):
-            queries = slice(p * PIECE_Q, (p + 1) * PIECE_Q)
-            nc.scalar.copy(val[:, queries, :], val_ps[p][:].rearrange("c (i t) -> c i t", t=T))
+        val_first = held.tile([P, PIECE_Q, T], F32, name="val_first")
+        nc.scalar.copy(val_first[:], val_ps[0][:].rearrange("c (i t) -> c i t", t=T))
+
+        def val_of(queries):
+            bank = val_ps[queries.start // PIECE_Q]
+            column = (queries.start % PIECE_Q) * T
+            return bank[:, column : column + CHUNK_Q * T].rearrange("c (i t) -> c i t", t=T)
 
         own_ps = psum.tile([P, T, HEADS], F32, name="own_ps", tag="bank")
         for t in range(T):
@@ -148,7 +151,7 @@ def tile_deepseekmla_kernel(tc, table, w, x_q, w_q, offs, out):
         for queries in chunks[: PIECE_Q // CHUNK_Q]:
             weigh(queries)
         first = slice(0, PIECE_Q)
-        nc.gpsimd.tensor_tensor(terms[:, first, :], val[:, first, :], weight[:, first, :], ALU.mult)
+        nc.gpsimd.tensor_tensor(terms[:, first, :], val_first[:], weight[:, first, :], ALU.mult)
         for width in (T // 2, T // 4, T // 8):
             nc.gpsimd.tensor_tensor(
                 terms[:, first, 0:width],
@@ -161,7 +164,7 @@ def tile_deepseekmla_kernel(tc, table, w, x_q, w_q, offs, out):
         for queries in chunks[PIECE_Q // CHUNK_Q :]:
             weigh(queries)
             nc.vector.tensor_tensor(
-                terms[:, queries, :], val[:, queries, :], weight[:, queries, :], ALU.mult
+                terms[:, queries, :], val_of(queries), weight[:, queries, :], ALU.mult
             )
             nc.vector.tensor_reduce(mix[:, queries], terms[:, queries, :], X, ALU.add)
 

@@ -17,6 +17,7 @@ PIECE = 512
 PIECE_Q = PIECE // T
 PIECES = QUERIES // PIECE_Q
 CHUNK_Q = 16
+HELPED = 1
 SCALE = 0.125
 
 FLOPS = 2 * P * 2 * P * QUERIES * T + 2 * P * P * QUERIES + 4 * P * QUERIES * T
@@ -88,8 +89,9 @@ def tile_deepseekmla_kernel(tc, table, w, x_q, w_q, offs, out):
                 prod_t[:, :, queries].rearrange("c (a b) i -> c a b i", a=T_OUT),
                 prod[:, :, queries, :].rearrange("c a i b -> c a b i"),
             )
-        val_first = held.tile([P, PIECE_Q, T], F32, name="val_first")
-        nc.scalar.copy(val_first[:], val_ps[0][:].rearrange("c (i t) -> c i t", t=T))
+        helped = slice(HELPED * PIECE_Q, (HELPED + 1) * PIECE_Q)
+        val_helped = held.tile([P, PIECE_Q, T], F32, name="val_helped")
+        nc.scalar.copy(val_helped[:], val_ps[HELPED][:].rearrange("c (i t) -> c i t", t=T))
 
         def val_of(queries):
             bank = val_ps[queries.start // PIECE_Q]
@@ -148,25 +150,18 @@ def tile_deepseekmla_kernel(tc, table, w, x_q, w_q, offs, out):
             )
             nc.scalar.activation(weight[:, queries, :], score_ps[:], EXP)
 
-        for queries in chunks[: PIECE_Q // CHUNK_Q]:
+        for queries in chunks:
             weigh(queries)
-        first = slice(0, PIECE_Q)
-        nc.gpsimd.tensor_tensor(terms[:, first, :], val_first[:], weight[:, first, :], ALU.mult)
-        for width in (T // 2, T // 4, T // 8):
-            nc.gpsimd.tensor_tensor(
-                terms[:, first, 0:width],
-                terms[:, first, 0:width],
-                terms[:, first, width : 2 * width],
-                ALU.add,
-            )
-        nc.gpsimd.tensor_tensor(mix[:, first], terms[:, first, 0], terms[:, first, 1], ALU.add)
-
-        for queries in chunks[PIECE_Q // CHUNK_Q :]:
-            weigh(queries)
-            nc.vector.tensor_tensor(
-                terms[:, queries, :], val_of(queries), weight[:, queries, :], ALU.mult
-            )
-            nc.vector.tensor_reduce(mix[:, queries], terms[:, queries, :], X, ALU.add)
+            if queries.start // PIECE_Q != HELPED:
+                nc.vector.tensor_tensor(
+                    terms[:, queries, :], val_of(queries), weight[:, queries, :], ALU.mult
+                )
+                nc.vector.tensor_reduce(mix[:, queries], terms[:, queries, :], X, ALU.add)
+            elif queries.stop == helped.stop:
+                nc.gpsimd.tensor_tensor(
+                    terms[:, helped, :], val_helped[:], weight[:, helped, :], ALU.mult
+                )
+        nc.vector.tensor_reduce(mix[:, helped], terms[:, helped, :], X, ALU.add)
 
         inv_ps = psum.tile([P, QUERIES], F32, name="inv_ps", tag="bank")
         nc.tensor.matmul(inv_ps[:], inv_wide[:], ident[:])

@@ -161,7 +161,13 @@ def tile_deepseekmla_kernel(tc, table, w, x_q, w_q, offs, out):
                 nc.gpsimd.tensor_tensor(
                     terms[:, helped, :], val_helped[:], weight[:, helped, :], ALU.mult
                 )
-        nc.vector.tensor_reduce(mix[:, helped], terms[:, helped, :], X, ALU.add)
+                nc.gpsimd.tensor_tensor(
+                    terms[:, helped, 0 : T // 2],
+                    terms[:, helped, 0 : T // 2],
+                    terms[:, helped, T // 2 : T],
+                    ALU.add,
+                )
+        nc.vector.tensor_reduce(mix[:, helped], terms[:, helped, 0 : T // 2], X, ALU.add)
 
         inv_ps = psum.tile([P, QUERIES], F32, name="inv_ps", tag="bank")
         nc.tensor.matmul(inv_ps[:], inv_wide[:], ident[:])

@@ -29,12 +29,12 @@ def tile_deepseekmla_kernel(tc, table, w, x_q, w_q, offs, out):
         tc.tile_pool(name="held", bufs=1) as held,
         tc.psum_pool(name="psum", bufs=8) as psum,
     ):
-        offsets = held.tile([P, QUERIES], U16, name="offsets")
-        nc.sync.dma_start(offsets[:], offs)
         table_sb = held.tile([P, PLACES], BF16, name="table_sb")
         nc.sync.dma_start(table_sb[:], table)
+        offsets = held.tile([P, QUERIES], U16, name="offsets")
+        nc.sync.dma_start(offsets[:], offs)
         w_sb = held.tile([P, 2 * P], BF16, name="w_sb")
-        nc.scalar.dma_start(w_sb[:], w)
+        nc.sync.dma_start(w_sb[:], w)
         w_q_sb = held.tile([P, P], BF16, name="w_q_sb")
         nc.scalar.dma_start(w_q_sb[:], w_q)
         x_q_sb = held.tile([P, QUERIES], BF16, name="x_q_sb")

@@ -112,13 +112,16 @@ def tile_deepseekmla_kernel(tc, table, w, x_q, w_q, offs, out):
             top[:].unsqueeze(2).to_broadcast(per_channel),
             -1.0,
         )
-        centred = held.tile([P, HEADS, T], F32, name="centred")
-        shift = minus_top[:].rearrange("i (h k) -> i h k", k=HEAD)[:, :, 0:1]
-        nc.vector.tensor_tensor(centred[:], own, shift.to_broadcast([P, HEADS, T]), ALU.add)
         own_exp = held.tile([P, HEADS, T], F32, name="own_exp")
-        nc.scalar.activation(own_exp[:], centred[:], EXP)
         total = held.tile([P, HEADS], F32, name="total")
-        nc.vector.tensor_reduce(total[:], own_exp[:], X, ALU.add)
+        for h in range(HEADS):
+            nc.scalar.activation(
+                own_exp[:, h, :],
+                own[:, h, :],
+                EXP,
+                bias=minus_top[:, h * HEAD : h * HEAD + 1],
+                accum_out=total[:, h : h + 1],
+            )
         inv = held.tile([P, HEADS], F32, name="inv")
         nc.vector.reciprocal(inv[:], total[:])
         inv_wide = held.tile([P, P], F32, name="inv_wide")

@@ -96,7 +96,8 @@ def tile_deepseekmla_kernel(tc, table, w, x_q, w_q, offs, out):
         def val_of(queries):
             bank = val_ps[queries.start // PIECE_Q]
             column = (queries.start % PIECE_Q) * T
-            return bank[:, column : column + CHUNK_Q * T].rearrange("c (i t) -> c i t", t=T)
+            columns = (queries.stop - queries.start) * T
+            return bank[:, column : column + columns].rearrange("c (i t) -> c i t", t=T)
 
         own_ps = psum.tile([P, T, HEADS], F32, name="own_ps", tag="bank")
         for t in range(T):
@@ -134,9 +135,12 @@ def tile_deepseekmla_kernel(tc, table, w, x_q, w_q, offs, out):
         terms = held.tile([P, QUERIES, T], F32, name="terms")
         mix = held.tile([P, QUERIES], F32, name="mix")
         chunks = [slice(k * CHUNK_Q, (k + 1) * CHUNK_Q) for k in range(QUERIES // CHUNK_Q)]
+        chunks = [queries for queries in chunks if queries.start // PIECE_Q != HELPED]
+        chunks.insert(HELPED * PIECE_Q // CHUNK_Q, helped)
 
         def weigh(queries):
-            score_ps = psum.tile([P, CHUNK_Q, T], F32, name="score_ps", tag="bank")
+            chunk_q = queries.stop - queries.start
+            score_ps = psum.tile([P, chunk_q, T], F32, name="score_ps", tag="bank")
             nc.tensor.matmul(
                 score_ps[:].rearrange("c i (a b) -> c i a b", a=T_OUT),
                 head_sum[:],
@@ -147,7 +151,7 @@ def tile_deepseekmla_kernel(tc, table, w, x_q, w_q, offs, out):
             nc.tensor.matmul(
                 score_ps[:],
                 minus_top[:],
-                ident_bf[:, queries].unsqueeze(2).to_broadcast([P, CHUNK_Q, T]),
+                ident_bf[:, queries].unsqueeze(2).to_broadcast([P, chunk_q, T]),
                 start=False,
                 stop=True,
             )
@@ -155,12 +159,12 @@ def tile_deepseekmla_kernel(tc, table, w, x_q, w_q, offs, out):
 
         for queries in chunks:
             weigh(queries)
-            if queries.start // PIECE_Q != HELPED:
+            if queries != helped:
                 nc.vector.tensor_tensor(
                     terms[:, queries, :], val_of(queries), weight[:, queries, :], ALU.mult
                 )
                 nc.vector.tensor_reduce(mix[:, queries], terms[:, queries, :], X, ALU.add)
-            elif queries.stop == helped.stop:
+            else:
                 nc.gpsimd.tensor_tensor(
                     terms[:, helped, :], val_helped[:], weight[:, helped, :], ALU.mult
                 )

@@ -31,10 +31,10 @@ def tile_deepseekmla_kernel(tc, table, w, x_q, w_q, offs, out):
     ):
         table_sb = held.tile([P, PLACES], BF16, name="table_sb")
         nc.sync.dma_start(table_sb[:], table)
-        offsets = held.tile([P, QUERIES], U16, name="offsets")
-        nc.sync.dma_start(offsets[:], offs)
         w_sb = held.tile([P, 2 * P], BF16, name="w_sb")
         nc.sync.dma_start(w_sb[:], w)
+        offsets = held.tile([P, QUERIES], U16, name="offsets")
+        nc.sync.dma_start(offsets[:], offs)
         w_q_sb = held.tile([P, P], BF16, name="w_q_sb")
         nc.scalar.dma_start(w_q_sb[:], w_q)
         x_q_sb = held.tile([P, QUERIES], BF16, name="x_q_sb")

import concourse.mybir as mybir
from concourse.masks import make_identity

BF16, F32, U16 = mybir.dt.bfloat16, mybir.dt.float32, mybir.dt.uint16
ALU = mybir.AluOpType
EXP = mybir.ActivationFunctionType.Exp
X = mybir.AxisListType.X

P = 128
PLACES = 1024
QUERIES = 128
T = 16
T_OUT, T_IN = 4, 4
HEADS = 2
HEAD = 64
PIECE = 512
PIECE_Q = PIECE // T
PIECES = QUERIES // PIECE_Q
CHUNK_Q = 16
HELPED = 1
SCALE = 0.125

FLOPS = 2 * P * 2 * P * QUERIES * T + 2 * P * P * QUERIES + 4 * P * QUERIES * T


def tile_deepseekmla_kernel(tc, table, w, x_q, w_q, offs, out):
    nc = tc.nc
    with (
        tc.tile_pool(name="held", bufs=1) as held,
        tc.psum_pool(name="psum", bufs=8) as psum,
    ):
        table_sb = held.tile([P, PLACES], BF16, name="table_sb")
        nc.sync.dma_start(table_sb[:], table)
        w_sb = held.tile([P, 2 * P], BF16, name="w_sb")
        nc.sync.dma_start(w_sb[:], w)
        offsets = held.tile([P, QUERIES], U16, name="offsets")
        nc.sync.dma_start(offsets[:], offs)
        w_q_sb = held.tile([P, P], BF16, name="w_q_sb")
        nc.scalar.dma_start(w_q_sb[:], w_q)
        x_q_sb = held.tile([P, QUERIES], BF16, name="x_q_sb")
        nc.scalar.dma_start(x_q_sb[:], x_q)

        head_sum = held.tile([P, P], BF16, name="head_sum")
        nc.gpsimd.memset(head_sum[:], 0.0)
        nc.gpsimd.memset(head_sum[0:HEAD, 0:HEAD], SCALE)
        nc.gpsimd.memset(head_sum[HEAD:P, HEAD:P], SCALE)
        head_pick = head_sum[:].rearrange("c (h k) -> c h k", k=HEAD)[:, :, 0]
        ident = held.tile([P, P], F32, name="ident")
        make_identity(nc, ident[:])
        ident_bf = held.tile([P, P], BF16, name="ident_bf")
        make_identity(nc, ident_bf[:])

        q_ps = psum.tile([P, QUERIES], F32, name="q_ps", tag="bank")
        nc.tensor.matmul(q_ps[:], w_q_sb[:], x_q_sb[:])
        q_sb = held.tile([P, QUERIES], F32, name="q_sb")
        nc.vector.tensor_copy(q_sb[:], q_ps[:])

        key_ps, val_ps = [], []
        for half, banks in ((0, key_ps), (1, val_ps)):
            for p in range(PIECES):
                bank = psum.tile([P, PIECE], F32, name=f"kv{half}_{p}", tag="bank")
                nc.tensor.matmul(
                    bank[:],
                    w_sb[:, half * P : (half + 1) * P],
                    table_sb[:].indirect(offsets[:, p * PIECE_Q : (p + 1) * PIECE_Q]),
                )
                banks.append(bank)

        by_query = [P, PIECE_Q, T]
        prod = held.tile([P, T_OUT, QUERIES, T_IN], BF16, name="prod")
        split_t = [P, PIECE_Q, T_OUT, T_IN]

        def prod_of(queries):
            return prod[:, :, queries, :].rearrange("c a i b -> c i a b")

        for p in range(PIECES):
            queries = slice(p * PIECE_Q, (p + 1) * PIECE_Q)
            nc.vector.tensor_tensor(
                prod_of(queries),
                key_ps[p][:].rearrange("c (i a b) -> c i a b", a=T_OUT, b=T_IN),
                q_sb[:, queries].unsqueeze(2).unsqueeze(3).to_broadcast(split_t),
                ALU.mult,
            )

        prod_t = held.tile([P, T, QUERIES], BF16, name="prod_t")
        for p in range(PIECES):
            queries = slice(p * PIECE_Q, (p + 1) * PIECE_Q)
            nc.scalar.copy(
                prod_t[:, :, queries].rearrange("c (a b) i -> c a b i", a=T_OUT),
                prod[:, :, queries, :].rearrange("c a i b -> c a b i"),
            )
        helped = slice(HELPED * PIECE_Q, (HELPED + 1) * PIECE_Q)
        val_helped = held.tile([P, PIECE_Q, T], F32, name="val_helped")
        nc.scalar.copy(val_helped[:], val_ps[HELPED][:].rearrange("c (i t) -> c i t", t=T))

        def val_of(queries):
            bank = val_ps[queries.start // PIECE_Q]
            column = (queries.start % PIECE_Q) * T
            columns = (queries.stop - queries.start) * T
            return bank[:, column : column + columns].rearrange("c (i t) -> c i t", t=T)

        own_ps = psum.tile([P, T, HEADS], F32, name="own_ps", tag="bank")
        for t in range(T):
            nc.tensor.matmul(own_ps[:, t, :], prod_t[:, t, :], head_pick)
        own = own_ps[:].rearrange("i t h -> i h t")
        per_channel = [P, HEADS, HEAD]

        top = held.tile([P, HEADS], F32, name="top")
        nc.vector.tensor_reduce(top[:], own, X, ALU.max)
        minus_top = held.tile([P, P], BF16, name="minus_top")
        nc.vector.tensor_scalar_mul(
            minus_top[:].rearrange("i (h k) -> i h k", k=HEAD),
            top[:].unsqueeze(2).to_broadcast(per_channel),
            -1.0,
        )
        own_exp = held.tile([P, HEADS, T], F32, name="own_exp")
        total = held.tile([P, HEADS], F32, name="total")
        for h in range(HEADS):
            nc.scalar.activation(
                own_exp[:, h, :],
                own[:, h, :],
                EXP,
                bias=minus_top[:, h * HEAD : h * HEAD + 1],
                accum_out=total[:, h : h + 1],
            )
        inv = held.tile([P, HEADS], F32, name="inv")
        nc.vector.reciprocal(inv[:], total[:])
        inv_wide = held.tile([P, P], F32, name="inv_wide")
        nc.vector.tensor_copy(
            inv_wide[:].rearrange("i (h k) -> i h k", k=HEAD),
            inv[:].unsqueeze(2).to_broadcast(per_channel),
        )

        weight = held.tile([P, QUERIES, T], F32, name="weight")
        terms = held.tile([P, QUERIES, T], F32, name="terms")
        mix = held.tile([P, QUERIES], F32, name="mix")
        chunks = [slice(k * CHUNK_Q, (k + 1) * CHUNK_Q) for k in range(QUERIES // CHUNK_Q)]
        chunks = [queries for queries in chunks if queries.start // PIECE_Q != HELPED]
        chunks.insert(HELPED * PIECE_Q // CHUNK_Q, helped)

        def weigh(queries):
            chunk_q = queries.stop - queries.start
            score_ps = psum.tile([P, chunk_q, T], F32, name="score_ps", tag="bank")
            nc.tensor.matmul(
                score_ps[:].rearrange("c i (a b) -> c i a b", a=T_OUT),
                head_sum[:],
                prod_of(queries),
                start=True,
                stop=False,
            )
            nc.tensor.matmul(
                score_ps[:],
                minus_top[:],
                ident_bf[:, queries].unsqueeze(2).to_broadcast([P, chunk_q, T]),
                start=False,
                stop=True,
            )
            nc.scalar.activation(weight[:, queries, :], score_ps[:], EXP)

        for queries in chunks:
            weigh(queries)
            if queries != helped:
                nc.vector.tensor_tensor(
                    terms[:, queries, :], val_of(queries), weight[:, queries, :], ALU.mult
                )
                nc.vector.tensor_reduce(mix[:, queries], terms[:, queries, :], X, ALU.add)
            else:
                nc.gpsimd.tensor_tensor(
                    terms[:, helped, :], val_helped[:], weight[:, helped, :], ALU.mult
                )
                nc.gpsimd.tensor_tensor(
                    terms[:, helped, 0 : T // 2],
                    terms[:, helped, 0 : T // 2],
                    terms[:, helped, T // 2 : T],
                    ALU.add,
                )
        nc.vector.tensor_reduce(mix[:, helped], terms[:, helped, 0 : T // 2], X, ALU.add)

        inv_ps = psum.tile([P, QUERIES], F32, name="inv_ps", tag="bank")
        nc.tensor.matmul(inv_ps[:], inv_wide[:], ident[:])
        out_sb = held.tile([P, QUERIES], F32, name="out_sb")
        nc.vector.tensor_tensor(out_sb[:], mix[:], inv_ps[:], ALU.mult)
        nc.sync.dma_start(out, out_sb[:])
